import numpy as np
import ml_dtypes


def mxq(x, axis, fmt="e4m3"):
    dtype, down = {"e4m3": (ml_dtypes.float8_e4m3fn, 7), "e5m2": (ml_dtypes.float8_e5m2, 14)}[fmt]
    v = np.moveaxis(np.asarray(x, np.float32).astype(ml_dtypes.bfloat16).astype(np.float64), axis, -1)
    blocks = v.reshape(v.shape[:-1] + (-1, 32))
    amax = np.abs(blocks).max(-1, keepdims=True)
    byte = np.maximum(np.where(amax > 0, np.frexp(amax)[1] - 1 + 127, 0) - down, 1)
    scale = np.exp2(byte - 127.0)
    codes = (blocks / scale).astype(np.float32).astype(dtype).astype(np.float64)
    return np.moveaxis((codes * scale).reshape(v.shape), -1, axis)


WIDE = False


def mx_kscale(k):
    if not WIDE:
        return np.ones(k)
    levels = np.array([10, -10, 5, -5, 0])
    a = np.random.permutation(np.resize(levels, k // 512 * 4)).reshape(k // 512, 4)
    idx = np.arange(k)
    return np.exp2(a[idx // 512, idx % 128 // 32])


BF16 = ml_dtypes.bfloat16


def bf(x):
    return np.asarray(x, np.float32).astype(BF16)


def f64(x):
    return np.asarray(x).astype(np.float64)


B, S, D, HD, M = 4, 1024, 2048, 128, 4
N = S // M
NEG = float(np.finfo(np.float32).min)


def prev(x):
    return np.concatenate([np.zeros_like(x[:, :1]), x[:, :-1]], axis=1)


def setup_inputs():
    s = mx_kscale(D)

    def w():
        return bf(np.random.standard_normal((D, HD)) / np.sqrt(D) / s[:, None])

    return {"h": bf(np.random.standard_normal((B, S, D)) * s),
            "w_kv_a": w(), "w_kv_b": w(), "w_z_a": w(), "w_z_b": w(),
            "b_a": bf(np.random.standard_normal((M, HD)) * 0.5),
            "b_b": bf(np.random.standard_normal((M, HD)) * 0.5)}


def reference(h, w_kv_a, w_kv_b, w_z_a, w_z_b, b_a, b_b):
    hq = mxq(f64(h), 2, "e4m3")
    c_a = (hq @ mxq(f64(w_kv_a), 0, "e4m3")).reshape(B, N, M, HD)
    c_b = (hq @ mxq(f64(w_kv_b), 0, "e4m3")).reshape(B, N, M, HD)
    z_a = (hq @ mxq(f64(w_z_a), 0, "e4m3")).reshape(B, N, M, HD)
    z_b = (hq @ mxq(f64(w_z_b), 0, "e4m3")).reshape(B, N, M, HD)
    logits = np.concatenate([prev(z_b) + f64(b_b), z_a + f64(b_a)], axis=2)
    valid = np.concatenate([np.broadcast_to((np.arange(N) > 0)[:, None], (N, M)), np.ones((N, M), bool)], axis=1)
    logits = np.where(valid[None, :, :, None], logits, NEG)
    e = np.exp(logits - logits.max(axis=2, keepdims=True))
    weights = e / e.sum(axis=2, keepdims=True)
    c_vals = np.concatenate([prev(c_b), c_a], axis=2)
    return np.sum(weights * c_vals, axis=2)

@@ -1,0 +1,337 @@
+from contextlib import ExitStack
+
+import concourse.mybir as mybir
+from concourse.masks import make_identity
+
+F32 = mybir.dt.float32
+BF16 = mybir.dt.bfloat16
+U32 = mybir.dt.uint32
+U8 = mybir.dt.uint8
+FP8X4 = mybir.dt.float8_e4m3fn_x4
+ACT = mybir.ActivationFunctionType
+
+P = 128
+PACK = 4
+K_PASS = P * PACK
+D = 2048
+PASSES = D // K_PASS
+FEATURES = 128
+BLOCK = 4
+WINDOW = 2 * BLOCK
+TILE_BLOCKS = P
+TOKENS = TILE_BLOCKS * BLOCK
+SEQUENCES = 4
+SEQ_TILES = 2
+TILES = SEQUENCES * SEQ_TILES
+HALF_K = D // 2
+HALF_WORDS = HALF_K // 2
+BANK_SQUARES = 4
+ROW = 264
+NEG = -3.4028234663852886e38
+AHEAD = 3
+
+FLOPS = 2 * SEQUENCES * 1024 * D * 4 * FEATURES
+
+
+def tile_tokenlevelcompressor_pa_kernel(tc, h, w_kv_a, w_kv_b, w_z_a, w_z_b, b_a, b_b, out):
+    nc = tc.nc
+    h_tiles = h.rearrange("n (t p i) k -> (n t) p i k", t=SEQ_TILES, p=P, i=BLOCK)
+    out_rows_of_tiles = out.rearrange("n (t j) f -> j (n t) f", t=SEQ_TILES)
+    weights = (w_z_b, w_z_a, w_kv_b, w_kv_a)
+    Z_B, Z_A, C_B, C_A = 0, 1, 2, 3
+    bank_names = ("z_b", "z_a", "c_b", "c_a")
+
+    with ExitStack() as ctx:
+        const = ctx.enter_context(tc.tile_pool(name="const", bufs=1))
+        hin = ctx.enter_context(tc.tile_pool(name="hin", bufs=2 * AHEAD))
+        grp = ctx.enter_context(tc.tile_pool(name="grp", bufs=PASSES))
+        quant = ctx.enter_context(tc.tile_pool(name="quant", bufs=2))
+        soft = ctx.enter_context(tc.tile_pool(name="soft", bufs=2))
+        tr_psum = ctx.enter_context(tc.psum_pool(name="tr_psum", bufs=4))
+        acc_psum = ctx.enter_context(tc.psum_pool(name="acc_psum", bufs=1))
+        ctx.enter_context(tc.manual_schedule())
+
+        h_half = {}
+        grouped = {}
+        h_codes = {}
+        h_scales = {}
+        banks = {}
+        top = {}
+        ep = {}
+
+        def load_h(t, half):
+            h_half[(t, half)] = hin.tile([P, BLOCK * HALF_K], BF16, name="h_half")
+            nc.sync.dma_start(
+                out=h_half[(t, half)][:].rearrange("p (i k) -> p i k", i=BLOCK),
+                in_=h_tiles[t][:, :, half * HALF_K : (half + 1) * HALF_K],
+            )
+
+        w_raw = const.tile([P, 4, PASSES, PACK, FEATURES], BF16, name="w_raw")
+
+        def load_weight(j):
+            nc.sync.dma_start(
+                out=w_raw[:, j].rearrange("p g (u e) c -> p (g u) (e c)", u=2, e=2),
+                in_=weights[j].rearrange("(s p e) c -> p s (e c)", s=2 * PASSES, p=P, e=2),
+            )
+
+        ident = const.tile([P, P], F32, name="ident")
+        make_identity(nc, ident[:])
+
+        table_seed = const.tile([P, 1], F32, name="table_seed")
+        table_out = const.tile([P, 1], F32, name="table_out")
+        nc.vector.memset(table_seed[:], 0.0)
+        nc.scalar.activation(out=table_out[:], in_=table_seed[:], func=ACT.Exp)
+
+        logits = [const.tile([P, WINDOW, ROW], F32, name="logits%d" % q) for q in range(2)]
+        values_b = [const.tile([P, BLOCK, ROW], F32, name="values_b%d" % q) for q in range(2)]
+        for q in range(2):
+            nc.vector.memset(logits[q][:, 0:BLOCK, 0:8], NEG)
+            nc.vector.memset(values_b[q][:, :, 0:8], 0.0)
+
+        bias_rows = const.tile([P, P], BF16, name="bias_rows")
+        bias_rows32 = const.tile([P, P], F32, name="bias_rows32")
+        bias = const.tile([P, WINDOW], F32, name="bias")
+        nc.vector.memset(bias_rows[:], 0.0)
+        nc.scalar.dma_start(out=bias_rows[0:BLOCK, :], in_=b_b)
+        nc.scalar.dma_start(out=bias_rows[BLOCK:WINDOW, :], in_=b_a)
+
+        def prepare_bias():
+            nc.vector.tensor_copy(out=bias_rows32[:], in_=bias_rows[:])
+            bias_bank = tr_psum.tile([P, BANK_SQUARES, P], F32, tag="tr", name="bias_bank")
+            nc.tensor.transpose(bias_bank[:, 0, :], bias_rows32[:], ident[:])
+            nc.vector.tensor_copy(out=bias[:], in_=bias_bank[:, 0, 0:WINDOW])
+
+        w_grouped = const.tile([P, 4, PASSES, FEATURES, PACK], BF16, name="w_grouped", align_bytes=64)
+        w_codes = const.tile([P, 4, PASSES, FEATURES], U32, name="w_codes", align_bytes=64)
+        w_scales = const.tile([P, 4, PASSES, FEATURES], U8, name="w_scales", align_bytes=64)
+
+        def regroup_weight(j):
+            nc.vector.tensor_copy(out=w_grouped[:, j], in_=w_raw[:, j].rearrange("p g t c -> p g c t"))
+
+        def quantise_weight(j):
+            nc.vector.quantize_mx(
+                out=w_codes[:, j].rearrange("p g c -> p (g c)").bitcast(FP8X4),
+                scales=w_scales[:, j].rearrange("p g c -> p (g c)"),
+                in_=w_grouped[:, j].rearrange("p g c t -> p (g c t)"),
+            )
+
+        def transpose_half(t, half):
+            if half == 0:
+                h_codes[t] = quant.tile([P, PASSES, TOKENS], U32, name="h_codes", align_bytes=64)
+                h_scales[t] = quant.tile([P, PASSES, TOKENS], U8, name="h_scales", align_bytes=64)
+            words = h_half[(t, half)][:].bitcast(F32)
+            for g_local in range(PASSES // 2):
+                g = half * (PASSES // 2) + g_local
+                grouped[(t, g)] = grp.tile([P, TOKENS * PACK], BF16, name="grouped", align_bytes=64)
+                grouped_words = grouped[(t, g)][:].bitcast(F32)
+                for pair in range(BLOCK // 2):
+                    bank = tr_psum.tile([P, 2, 2, P], F32, tag="tr", name="bank")
+                    for a in range(2):
+                        for u in range(2):
+                            first = (2 * pair + a) * HALF_WORDS + g_local * 2 * P + u * P
+                            nc.tensor.transpose(bank[:, a, u, :], words[:, first : first + P], ident[:])
+                    nc.scalar.copy(
+                        out=grouped_words[:, pair * 4 * P : (pair + 1) * 4 * P].rearrange(
+                            "p (a r u) -> p a r u", a=2, u=2
+                        ),
+                        in_=bank[:].rearrange("p a u r -> p a r u"),
+                    )
+            if t + AHEAD < TILES:
+                load_h(t + AHEAD, half)
+
+        def quantise_h(t, g):
+            nc.vector.quantize_mx(
+                out=h_codes[t][:, g, :].bitcast(FP8X4),
+                scales=h_scales[t][:, g, :],
+                in_=grouped[(t, g)][:],
+            )
+
+        def project(t, j):
+            banks[(t, j)] = acc_psum.tile([P, TOKENS], F32, tag=bank_names[j], name=bank_names[j])
+            for g in range(PASSES):
+                nc.tensor.matmul_mx(
+                    out=banks[(t, j)][:],
+                    lhsT=w_codes[:, j, g, :].bitcast(FP8X4),
+                    lhsT_scale=w_scales[:, j, g, :],
+                    rhs=h_codes[t][:, g, :].bitcast(FP8X4),
+                    rhs_scale=h_scales[t][:, g, :],
+                    start=(g == 0),
+                    stop=(g == PASSES - 1),
+                )
+
+        def place(t):
+            return (t // SEQ_TILES) % 2, (t % SEQ_TILES) * TILE_BLOCKS
+
+        def move_logits(t):
+            q, first = place(t)
+            for i in range(BLOCK):
+                nc.scalar.activation(
+                    out=logits[q][:, i, first + 1 : first + 1 + TILE_BLOCKS],
+                    in_=banks[(t, Z_B)][:, i * TILE_BLOCKS : (i + 1) * TILE_BLOCKS],
+                    func=ACT.Identity,
+                    bias=bias[:, i : i + 1],
+                    scale=1.0,
+                )
+            for i in range(BLOCK):
+                nc.scalar.activation(
+                    out=logits[q][:, BLOCK + i, first : first + TILE_BLOCKS],
+                    in_=banks[(t, Z_A)][:, i * TILE_BLOCKS : (i + 1) * TILE_BLOCKS],
+                    func=ACT.Identity,
+                    bias=bias[:, BLOCK + i : BLOCK + i + 1],
+                    scale=1.0,
+                )
+
+        def move_values_b(t):
+            q, first = place(t)
+            nc.scalar.copy(
+                out=values_b[q][:, :, first + 1 : first + 1 + TILE_BLOCKS],
+                in_=banks[(t, C_B)][:].rearrange("p (i j) -> p i j", i=BLOCK),
+            )
+
+        def max_first(t):
+            q, first = place(t)
+            top[t] = soft.tile([P, BLOCK, TILE_BLOCKS], F32, name="top")
+            nc.vector.tensor_max(
+                out=top[t][:],
+                in0=logits[q][:, 0:BLOCK, first : first + TILE_BLOCKS],
+                in1=logits[q][:, BLOCK:WINDOW, first : first + TILE_BLOCKS],
+            )
+
+        def max_fold(t, n):
+            nc.vector.tensor_max(out=top[t][:, 0:n, :], in0=top[t][:, 0:n, :], in1=top[t][:, n : 2 * n, :])
+
+        def subtract_max(t):
+            q, first = place(t)
+            ep[t] = soft.tile([P, 2, WINDOW, TILE_BLOCKS], F32, name="ep")
+            nc.vector.tensor_sub(
+                out=ep[t][:, 0],
+                in0=logits[q][:, :, first : first + TILE_BLOCKS],
+                in1=top[t][:, 0:1, :].to_broadcast([P, WINDOW, TILE_BLOCKS]),
+            )
+
+        def exponentials(t):
+            nc.scalar.activation(out=ep[t][:, 0], in_=ep[t][:, 0], func=ACT.Exp)
+
+        def weigh(t):
+            q, first = place(t)
+            nc.vector.tensor_mul(
+                out=ep[t][:, 1, BLOCK:WINDOW],
+                in0=ep[t][:, 0, BLOCK:WINDOW],
+                in1=banks[(t, C_A)][:].rearrange("p (i j) -> p i j", i=BLOCK),
+            )
+            nc.vector.tensor_mul(
+                out=ep[t][:, 1, 0:BLOCK],
+                in0=ep[t][:, 0, 0:BLOCK],
+                in1=values_b[q][:, :, first : first + TILE_BLOCKS],
+            )
+
+        def add_fold(t, n):
+            nc.vector.tensor_add(out=ep[t][:, :, 0:n], in0=ep[t][:, :, 0:n], in1=ep[t][:, :, n : 2 * n])
+
+        sums = const.tile([P, 2, TILES * TILE_BLOCKS], F32, name="sums")
+        inverse_root = const.tile([P, TILES * TILE_BLOCKS], F32, name="inverse_root")
+        inverse = const.tile([P, TILES * TILE_BLOCKS], F32, name="inverse")
+        result = const.tile([P, TILES * TILE_BLOCKS], F32, name="result")
+
+        def add_last(t):
+            nc.vector.tensor_add(
+                out=sums[:, :, t * TILE_BLOCKS : (t + 1) * TILE_BLOCKS], in0=ep[t][:, :, 0, :], in1=ep[t][:, :, 1, :]
+            )
+
+        def invert(t_from, t_to):
+            cols = slice(t_from * TILE_BLOCKS, t_to * TILE_BLOCKS)
+            nc.scalar.activation(out=inverse_root[:, cols], in_=sums[:, 0, cols], func=ACT.Abs_reciprocal_sqrt)
+            nc.scalar.activation(out=inverse[:, cols], in_=inverse_root[:, cols], func=ACT.Square)
+
+        def divide(t_from, t_to):
+            cols = slice(t_from * TILE_BLOCKS, t_to * TILE_BLOCKS)
+            nc.vector.tensor_mul(out=result[:, cols], in0=sums[:, 1, cols], in1=inverse[:, cols])
+
+        out_bank = {}
+
+        def transpose_out(t_from):
+            out_bank[t_from] = tr_psum.tile([P, BANK_SQUARES, FEATURES], F32, tag="tr", name="out_bank")
+            for n in range(BANK_SQUARES):
+                t = t_from + n
+                nc.tensor.transpose(
+                    out_bank[t_from][:, n, :], result[:, t * TILE_BLOCKS : (t + 1) * TILE_BLOCKS], ident[:]
+                )
+
+        def store(t_from):
+            out_rows = soft.tile([P, BANK_SQUARES, FEATURES], F32, name="out_rows")
+            nc.scalar.copy(out=out_rows[:], in_=out_bank[t_from][:])
+            nc.sync.dma_start(out=out_rows_of_tiles[:, t_from : t_from + BANK_SQUARES, :], in_=out_rows[:])
+
+        load_h(0, 0)
+        load_h(0, 1)
+        load_weight(Z_B)
+        load_weight(Z_A)
+        load_h(1, 0)
+        load_weight(C_B)
+        load_weight(C_A)
+        load_h(1, 1)
+        load_h(2, 0)
+        load_h(2, 1)
+        prepare_bias()
+
+        transpose_half(0, 0)
+        quantise_h(0, 0)
+        quantise_h(0, 1)
+        regroup_weight(Z_B)
+        transpose_half(0, 1)
+        quantise_h(0, 2)
+        regroup_weight(Z_A)
+        quantise_weight(Z_B)
+        quantise_h(0, 3)
+        quantise_weight(Z_A)
+        regroup_weight(C_B)
+        regroup_weight(C_A)
+        quantise_weight(C_B)
+        quantise_weight(C_A)
+
+        for s in range(1, TILES + 1):
+            a, b, c = s, s - 1, s - 2
+            if c >= 0:
+                weigh(c)
+            if a < TILES:
+                transpose_half(a, 0)
+                quantise_h(a, 0)
+            if c >= 0:
+                add_fold(c, 4)
+            if a < TILES:
+                quantise_h(a, 1)
+            project(b, Z_B)
+            project(b, Z_A)
+            move_logits(b)
+            if a < TILES:
+                transpose_half(a, 1)
+            if c >= 0:
+                add_fold(c, 2)
+            max_first(b)
+            if c >= 0:
+                add_last(c)
+            max_fold(b, 2)
+            max_fold(b, 1)
+            subtract_max(b)
+            project(b, C_B)
+            project(b, C_A)
+            exponentials(b)
+            move_values_b(b)
+            if a < TILES:
+                quantise_h(a, 2)
+                quantise_h(a, 3)
+
+        last = TILES - 1
+        invert(0, BANK_SQUARES)
+        invert(BANK_SQUARES, last)
+        weigh(last)
+        add_fold(last, 4)
+        add_fold(last, 2)
+        divide(0, BANK_SQUARES)
+        add_last(last)
+        transpose_out(0)
+        invert(last, TILES)
+        divide(BANK_SQUARES, TILES)
+        store(0)
+        transpose_out(BANK_SQUARES)
+        store(BANK_SQUARES)

@@ -74,6 +74,13 @@ def tile_tokenlevelcompressor_pa_kernel(tc, h, w_kv_a, w_kv_b, w_z_a, w_z_b, b_a
                 in_=weights[j].rearrange("(s p e) c -> p s (e c)", s=2 * PASSES, p=P, e=2),
             )
 
+        bias_rows = const.tile([P, P], BF16, name="bias_rows")
+        bias_rows32 = const.tile([P, P], F32, name="bias_rows32")
+        bias = const.tile([P, WINDOW], F32, name="bias")
+        nc.vector.memset(bias_rows[:], 0.0)
+        nc.sync.dma_start(out=bias_rows[0:BLOCK, :], in_=b_b)
+        nc.sync.dma_start(out=bias_rows[BLOCK:WINDOW, :], in_=b_a)
+
         ident = const.tile([P, P], F32, name="ident")
         make_identity(nc, ident[:])
 
@@ -87,13 +94,6 @@ def tile_tokenlevelcompressor_pa_kernel(tc, h, w_kv_a, w_kv_b, w_z_a, w_z_b, b_a
         for q in range(2):
             nc.vector.memset(logits[q][:, 0:BLOCK, 0:8], NEG)
             nc.vector.memset(values_b[q][:, :, 0:8], 0.0)
-
-        bias_rows = const.tile([P, P], BF16, name="bias_rows")
-        bias_rows32 = const.tile([P, P], F32, name="bias_rows32")
-        bias = const.tile([P, WINDOW], F32, name="bias")
-        nc.vector.memset(bias_rows[:], 0.0)
-        nc.scalar.dma_start(out=bias_rows[0:BLOCK, :], in_=b_b)
-        nc.scalar.dma_start(out=bias_rows[BLOCK:WINDOW, :], in_=b_a)
 
         def prepare_bias():
             nc.vector.tensor_copy(out=bias_rows32[:], in_=bias_rows[:])
@@ -212,13 +212,15 @@ def tile_tokenlevelcompressor_pa_kernel(tc, h, w_kv_a, w_kv_b, w_z_a, w_z_b, b_a
         def exponentials(t):
             nc.scalar.activation(out=ep[t][:, 0], in_=ep[t][:, 0], func=ACT.Exp)
 
-        def weigh(t):
-            q, first = place(t)
+        def weigh_a(t):
             nc.vector.tensor_mul(
                 out=ep[t][:, 1, BLOCK:WINDOW],
                 in0=ep[t][:, 0, BLOCK:WINDOW],
                 in1=banks[(t, C_A)][:].rearrange("p (i j) -> p i j", i=BLOCK),
             )
+
+        def weigh_b(t):
+            q, first = place(t)
             nc.vector.tensor_mul(
                 out=ep[t][:, 1, 0:BLOCK],
                 in0=ep[t][:, 0, 0:BLOCK],
@@ -289,49 +291,59 @@ def tile_tokenlevelcompressor_pa_kernel(tc, h, w_kv_a, w_kv_b, w_z_a, w_z_b, b_a
         quantise_weight(C_B)
         quantise_weight(C_A)
 
-        for s in range(1, TILES + 1):
-            a, b, c = s, s - 1, s - 2
-            if c >= 0:
-                weigh(c)
-            if a < TILES:
+        def live(t):
+            return 0 <= t < TILES
+
+        for s in range(1, TILES + 2):
+            a, b, c, d = s, s - 1, s - 2, s - 3
+            if live(c):
+                subtract_max(c)
+            if live(a):
                 transpose_half(a, 0)
                 quantise_h(a, 0)
-            if c >= 0:
-                add_fold(c, 4)
-            if a < TILES:
                 quantise_h(a, 1)
-            project(b, Z_B)
-            project(b, Z_A)
-            move_logits(b)
-            if a < TILES:
+            if live(c):
+                exponentials(c)
+            if live(b):
+                project(b, Z_B)
+                project(b, Z_A)
+                move_logits(b)
+            if live(d):
+                add_fold(d, 2)
+            if live(c):
+                weigh_a(c)
+            if live(d):
+                add_last(d)
+            if live(c):
+                weigh_b(c)
+            if live(a):
                 transpose_half(a, 1)
-            if c >= 0:
-                add_fold(c, 2)
-            max_first(b)
-            if c >= 0:
-                add_last(c)
-            max_fold(b, 2)
-            max_fold(b, 1)
-            subtract_max(b)
-            project(b, C_B)
-            project(b, C_A)
-            exponentials(b)
-            move_values_b(b)
-            if a < TILES:
+            if live(b):
+                max_first(b)
+            if live(c):
+                add_fold(c, 4)
+            if live(b):
+                max_fold(b, 2)
+            if live(a):
                 quantise_h(a, 2)
+            if live(b):
+                max_fold(b, 1)
+            if live(a):
                 quantise_h(a, 3)
+            if live(b):
+                project(b, C_B)
+                project(b, C_A)
+                move_values_b(b)
 
         last = TILES - 1
         invert(0, BANK_SQUARES)
         invert(BANK_SQUARES, last)
-        weigh(last)
-        add_fold(last, 4)
-        add_fold(last, 2)
         divide(0, BANK_SQUARES)
-        add_last(last)
+        add_fold(last, 2)
         transpose_out(0)
+        add_last(last)
+        store(0)
         invert(last, TILES)
         divide(BANK_SQUARES, TILES)
-        store(0)
         transpose_out(BANK_SQUARES)
         store(BANK_SQUARES)

@@ -49,7 +49,6 @@ def tile_tokenlevelcompressor_pa_kernel(tc, h, w_kv_a, w_kv_b, w_z_a, w_z_b, b_a
         soft = ctx.enter_context(tc.tile_pool(name="soft", bufs=2))
         tr_psum = ctx.enter_context(tc.psum_pool(name="tr_psum", bufs=4))
         acc_psum = ctx.enter_context(tc.psum_pool(name="acc_psum", bufs=1))
-        ctx.enter_context(tc.manual_schedule())
 
         h_half = {}
         grouped = {}

@@ -23,8 +23,9 @@ TOKENS = TILE_BLOCKS * BLOCK
 SEQUENCES = 4
 SEQ_TILES = 2
 TILES = SEQUENCES * SEQ_TILES
-HALF_K = D // 2
-HALF_WORDS = HALF_K // 2
+HALF = BLOCK // 2
+WORDS = D // 2
+HALF_TOKENS = HALF * TILE_BLOCKS
 BANK_SQUARES = 4
 ROW = 264
 NEG = -3.4028234663852886e38
@@ -44,11 +45,12 @@ def tile_tokenlevelcompressor_pa_kernel(tc, h, w_kv_a, w_kv_b, w_z_a, w_z_b, b_a
     with ExitStack() as ctx:
         const = ctx.enter_context(tc.tile_pool(name="const", bufs=1))
         hin = ctx.enter_context(tc.tile_pool(name="hin", bufs=2 * AHEAD))
-        grp = ctx.enter_context(tc.tile_pool(name="grp", bufs=PASSES))
+        grp = ctx.enter_context(tc.tile_pool(name="grp", bufs=2 * PASSES))
         quant = ctx.enter_context(tc.tile_pool(name="quant", bufs=2))
         soft = ctx.enter_context(tc.tile_pool(name="soft", bufs=2))
         tr_psum = ctx.enter_context(tc.psum_pool(name="tr_psum", bufs=4))
         acc_psum = ctx.enter_context(tc.psum_pool(name="acc_psum", bufs=1))
+        ctx.enter_context(tc.manual_schedule())
 
         h_half = {}
         grouped = {}
@@ -59,10 +61,10 @@ def tile_tokenlevelcompressor_pa_kernel(tc, h, w_kv_a, w_kv_b, w_z_a, w_z_b, b_a
         ep = {}
 
         def load_h(t, half):
-            h_half[(t, half)] = hin.tile([P, BLOCK * HALF_K], BF16, name="h_half")
+            h_half[(t, half)] = hin.tile([P, HALF * D], BF16, name="h_half")
             nc.sync.dma_start(
-                out=h_half[(t, half)][:].rearrange("p (i k) -> p i k", i=BLOCK),
-                in_=h_tiles[t][:, :, half * HALF_K : (half + 1) * HALF_K],
+                out=h_half[(t, half)][:].rearrange("p (i k) -> p i k", i=HALF),
+                in_=h_tiles[t][:, half * HALF : (half + 1) * HALF, :],
             )
 
         w_raw = const.tile([P, 4, PASSES, PACK, FEATURES], BF16, name="w_raw")
@@ -77,8 +79,6 @@ def tile_tokenlevelcompressor_pa_kernel(tc, h, w_kv_a, w_kv_b, w_z_a, w_z_b, b_a
         bias_rows32 = const.tile([P, P], F32, name="bias_rows32")
         bias = const.tile([P, WINDOW], F32, name="bias")
         nc.vector.memset(bias_rows[:], 0.0)
-        nc.sync.dma_start(out=bias_rows[0:BLOCK, :], in_=b_b)
-        nc.sync.dma_start(out=bias_rows[BLOCK:WINDOW, :], in_=b_a)
 
         ident = const.tile([P, P], F32, name="ident")
         make_identity(nc, ident[:])
@@ -119,31 +119,29 @@ def tile_tokenlevelcompressor_pa_kernel(tc, h, w_kv_a, w_kv_b, w_z_a, w_z_b, b_a
                 h_codes[t] = quant.tile([P, PASSES, TOKENS], U32, name="h_codes", align_bytes=64)
                 h_scales[t] = quant.tile([P, PASSES, TOKENS], U8, name="h_scales", align_bytes=64)
             words = h_half[(t, half)][:].bitcast(F32)
-            for g_local in range(PASSES // 2):
-                g = half * (PASSES // 2) + g_local
-                grouped[(t, g)] = grp.tile([P, TOKENS * PACK], BF16, name="grouped", align_bytes=64)
-                grouped_words = grouped[(t, g)][:].bitcast(F32)
-                for pair in range(BLOCK // 2):
-                    bank = tr_psum.tile([P, 2, 2, P], F32, tag="tr", name="bank")
-                    for a in range(2):
-                        for u in range(2):
-                            first = (2 * pair + a) * HALF_WORDS + g_local * 2 * P + u * P
-                            nc.tensor.transpose(bank[:, a, u, :], words[:, first : first + P], ident[:])
-                    nc.scalar.copy(
-                        out=grouped_words[:, pair * 4 * P : (pair + 1) * 4 * P].rearrange(
-                            "p (a r u) -> p a r u", a=2, u=2
-                        ),
-                        in_=bank[:].rearrange("p a u r -> p a r u"),
-                    )
+            for g in range(PASSES):
+                bank = tr_psum.tile([P, HALF, 2, P], F32, tag="tr", name="bank")
+                for a in range(HALF):
+                    for u in range(2):
+                        first = a * WORDS + g * 2 * P + u * P
+                        nc.tensor.transpose(bank[:, a, u, :], words[:, first : first + P], ident[:])
+                grouped[(t, half, g)] = grp.tile([P, HALF_TOKENS * PACK], BF16, name="grouped", align_bytes=64)
+                nc.scalar.copy(
+                    out=grouped[(t, half, g)][:].bitcast(F32).rearrange("p (a r u) -> p a r u", a=HALF, u=2),
+                    in_=bank[:].rearrange("p a u r -> p a r u"),
+                )
             if t + AHEAD < TILES:
                 load_h(t + AHEAD, half)
 
-        def quantise_h(t, g):
-            nc.vector.quantize_mx(
-                out=h_codes[t][:, g, :].bitcast(FP8X4),
-                scales=h_scales[t][:, g, :],
-                in_=grouped[(t, g)][:],
-            )
+        def quantise_h(t, quarter):
+            half, pass_pair = divmod(quarter, 2)
+            cols = slice(half * HALF_TOKENS, (half + 1) * HALF_TOKENS)
+            for g in (2 * pass_pair, 2 * pass_pair + 1):
+                nc.vector.quantize_mx(
+                    out=h_codes[t][:, g, cols].bitcast(FP8X4),
+                    scales=h_scales[t][:, g, cols],
+                    in_=grouped[(t, half, g)][:],
+                )
 
         def project(t, j):
             banks[(t, j)] = acc_psum.tile([P, TOKENS], F32, tag=bank_names[j], name=bank_names[j])
@@ -250,21 +248,22 @@ def tile_tokenlevelcompressor_pa_kernel(tc, h, w_kv_a, w_kv_b, w_z_a, w_z_b, b_a
 
         out_bank = {}
 
-        def transpose_out(t_from):
+        def transpose_out(t_from, t_to):
             out_bank[t_from] = tr_psum.tile([P, BANK_SQUARES, FEATURES], F32, tag="tr", name="out_bank")
-            for n in range(BANK_SQUARES):
-                t = t_from + n
+            for t in range(t_from, t_to):
                 nc.tensor.transpose(
-                    out_bank[t_from][:, n, :], result[:, t * TILE_BLOCKS : (t + 1) * TILE_BLOCKS], ident[:]
+                    out_bank[t_from][:, t - t_from, :], result[:, t * TILE_BLOCKS : (t + 1) * TILE_BLOCKS], ident[:]
                 )
 
-        def store(t_from):
-            out_rows = soft.tile([P, BANK_SQUARES, FEATURES], F32, name="out_rows")
-            nc.scalar.copy(out=out_rows[:], in_=out_bank[t_from][:])
-            nc.sync.dma_start(out=out_rows_of_tiles[:, t_from : t_from + BANK_SQUARES, :], in_=out_rows[:])
+        def store(t_from, t_to):
+            out_rows = const.tile([P, t_to - t_from, FEATURES], F32, name="out_rows%d" % t_from)
+            nc.scalar.copy(out=out_rows[:], in_=out_bank[t_from][:, 0 : t_to - t_from, :])
+            nc.sync.dma_start(out=out_rows_of_tiles[:, t_from:t_to, :], in_=out_rows[:])
 
         load_h(0, 0)
         load_h(0, 1)
+        nc.sync.dma_start(out=bias_rows[0:BLOCK, :], in_=b_b)
+        nc.sync.dma_start(out=bias_rows[BLOCK:WINDOW, :], in_=b_a)
         load_weight(Z_B)
         load_weight(Z_A)
         load_h(1, 0)
@@ -273,13 +272,13 @@ def tile_tokenlevelcompressor_pa_kernel(tc, h, w_kv_a, w_kv_b, w_z_a, w_z_b, b_a
         load_h(1, 1)
         load_h(2, 0)
         load_h(2, 1)
-        prepare_bias()
 
         transpose_half(0, 0)
         quantise_h(0, 0)
         quantise_h(0, 1)
         regroup_weight(Z_B)
         transpose_half(0, 1)
+        prepare_bias()
         quantise_h(0, 2)
         regroup_weight(Z_A)
         quantise_weight(Z_B)
@@ -339,10 +338,13 @@ def tile_tokenlevelcompressor_pa_kernel(tc, h, w_kv_a, w_kv_b, w_z_a, w_z_b, b_a
         invert(BANK_SQUARES, last)
         divide(0, BANK_SQUARES)
         add_fold(last, 2)
-        transpose_out(0)
+        transpose_out(0, BANK_SQUARES)
+        store(0, BANK_SQUARES)
+        divide(BANK_SQUARES, last)
         add_last(last)
-        store(0)
+        transpose_out(BANK_SQUARES, last)
         invert(last, TILES)
-        divide(BANK_SQUARES, TILES)
-        transpose_out(BANK_SQUARES)
-        store(BANK_SQUARES)
+        store(BANK_SQUARES, last)
+        divide(last, TILES)
+        transpose_out(last, TILES)
+        store(last, TILES)

@@ -46,7 +46,7 @@ def tile_tokenlevelcompressor_pa_kernel(tc, h, w_kv_a, w_kv_b, w_z_a, w_z_b, b_a
         const = ctx.enter_context(tc.tile_pool(name="const", bufs=1))
         hin = ctx.enter_context(tc.tile_pool(name="hin", bufs=2 * AHEAD))
         grp = ctx.enter_context(tc.tile_pool(name="grp", bufs=2 * PASSES))
-        quant = ctx.enter_context(tc.tile_pool(name="quant", bufs=2))
+        quant = ctx.enter_context(tc.tile_pool(name="quant", bufs=3))
         soft = ctx.enter_context(tc.tile_pool(name="soft", bufs=2))
         tr_psum = ctx.enter_context(tc.psum_pool(name="tr_psum", bufs=4))
         acc_psum = ctx.enter_context(tc.psum_pool(name="acc_psum", bufs=1))
@@ -89,10 +89,10 @@ def tile_tokenlevelcompressor_pa_kernel(tc, h, w_kv_a, w_kv_b, w_z_a, w_z_b, b_a
         nc.scalar.activation(out=table_out[:], in_=table_seed[:], func=ACT.Exp)
 
         logits = [const.tile([P, WINDOW, ROW], F32, name="logits%d" % q) for q in range(2)]
-        values_b = [const.tile([P, BLOCK, ROW], F32, name="values_b%d" % q) for q in range(2)]
+        carry = [const.tile([P, BLOCK, 1], F32, name="carry%d" % q) for q in range(2)]
+        nc.vector.memset(carry[0][:], 0.0)
         for q in range(2):
             nc.vector.memset(logits[q][:, 0:BLOCK, 0:8], NEG)
-            nc.vector.memset(values_b[q][:, :, 0:8], 0.0)
 
         def prepare_bias():
             nc.vector.tensor_copy(out=bias_rows32[:], in_=bias_rows[:])
@@ -178,11 +178,10 @@ def tile_tokenlevelcompressor_pa_kernel(tc, h, w_kv_a, w_kv_b, w_z_a, w_z_b, b_a
                     scale=1.0,
                 )
 
-        def move_values_b(t):
-            q, first = place(t)
+        def keep_last_values_b(t):
             nc.scalar.copy(
-                out=values_b[q][:, :, first + 1 : first + 1 + TILE_BLOCKS],
-                in_=banks[(t, C_B)][:].rearrange("p (i j) -> p i j", i=BLOCK),
+                out=carry[1][:],
+                in_=banks[(t, C_B)][:].rearrange("p (i j) -> p i j", i=BLOCK)[:, :, TILE_BLOCKS - 1 : TILE_BLOCKS],
             )
 
         def max_first(t):
@@ -217,11 +216,15 @@ def tile_tokenlevelcompressor_pa_kernel(tc, h, w_kv_a, w_kv_b, w_z_a, w_z_b, b_a
             )
 
         def weigh_b(t):
-            q, first = place(t)
             nc.vector.tensor_mul(
-                out=ep[t][:, 1, 0:BLOCK],
-                in0=ep[t][:, 0, 0:BLOCK],
-                in1=values_b[q][:, :, first : first + TILE_BLOCKS],
+                out=ep[t][:, 1, 0:BLOCK, 1:TILE_BLOCKS],
+                in0=ep[t][:, 0, 0:BLOCK, 1:TILE_BLOCKS],
+                in1=banks[(t, C_B)][:].rearrange("p (i j) -> p i j", i=BLOCK)[:, :, 0 : TILE_BLOCKS - 1],
+            )
+
+        def weigh_b_first(t):
+            nc.vector.tensor_mul(
+                out=ep[t][:, 1, 0:BLOCK, 0:1], in0=ep[t][:, 0, 0:BLOCK, 0:1], in1=carry[t % SEQ_TILES][:]
             )
 
         def add_fold(t, n):
@@ -292,46 +295,47 @@ def tile_tokenlevelcompressor_pa_kernel(tc, h, w_kv_a, w_kv_b, w_z_a, w_z_b, b_a
         def live(t):
             return 0 <= t < TILES
 
-        for s in range(1, TILES + 2):
+        for s in range(1, TILES + 3):
             a, b, c, d = s, s - 1, s - 2, s - 3
-            if live(c):
-                subtract_max(c)
+            if live(d):
+                weigh_a(d)
+                weigh_b(d)
+                weigh_b_first(d)
             if live(a):
                 transpose_half(a, 0)
                 quantise_h(a, 0)
+            if live(d):
+                add_fold(d, 4)
+            if live(a):
                 quantise_h(a, 1)
-            if live(c):
-                exponentials(c)
             if live(b):
                 project(b, Z_B)
                 project(b, Z_A)
                 move_logits(b)
-            if live(d):
+            if live(c):
+                subtract_max(c)
+            if live(d) and d < TILES - 1:
                 add_fold(d, 2)
-            if live(c):
-                weigh_a(c)
-            if live(d):
-                add_last(d)
-            if live(c):
-                weigh_b(c)
             if live(a):
                 transpose_half(a, 1)
             if live(b):
                 max_first(b)
-            if live(c):
-                add_fold(c, 4)
-            if live(b):
-                max_fold(b, 2)
+            if live(d) and d < TILES - 1:
+                add_last(d)
             if live(a):
                 quantise_h(a, 2)
             if live(b):
-                max_fold(b, 1)
+                max_fold(b, 2)
             if live(a):
                 quantise_h(a, 3)
             if live(b):
-                project(b, C_B)
-                project(b, C_A)
-                move_values_b(b)
+                max_fold(b, 1)
+            if live(c):
+                project(c, C_B)
+                project(c, C_A)
+                exponentials(c)
+                if c % SEQ_TILES == 0:
+                    keep_last_values_b(c)
 
         last = TILES - 1
         invert(0, BANK_SQUARES)

@@ -47,7 +47,7 @@ def tile_tokenlevelcompressor_pa_kernel(tc, h, w_kv_a, w_kv_b, w_z_a, w_z_b, b_a
         hin = ctx.enter_context(tc.tile_pool(name="hin", bufs=2 * AHEAD))
         grp = ctx.enter_context(tc.tile_pool(name="grp", bufs=2 * PASSES))
         quant = ctx.enter_context(tc.tile_pool(name="quant", bufs=3))
-        soft = ctx.enter_context(tc.tile_pool(name="soft", bufs=2))
+        soft = ctx.enter_context(tc.tile_pool(name="soft", bufs=3))
         tr_psum = ctx.enter_context(tc.psum_pool(name="tr_psum", bufs=4))
         acc_psum = ctx.enter_context(tc.psum_pool(name="acc_psum", bufs=1))
         ctx.enter_context(tc.manual_schedule())
@@ -235,6 +235,9 @@ def tile_tokenlevelcompressor_pa_kernel(tc, h, w_kv_a, w_kv_b, w_z_a, w_z_b, b_a
         inverse = const.tile([P, TILES * TILE_BLOCKS], F32, name="inverse")
         result = const.tile([P, TILES * TILE_BLOCKS], F32, name="result")
 
+        def add_fold_on_gpsimd(t, n):
+            nc.gpsimd.tensor_add(out=ep[t][:, :, 0:n], in0=ep[t][:, :, 0:n], in1=ep[t][:, :, n : 2 * n])
+
         def add_last(t):
             nc.vector.tensor_add(
                 out=sums[:, :, t * TILE_BLOCKS : (t + 1) * TILE_BLOCKS], in0=ep[t][:, :, 0, :], in1=ep[t][:, :, 1, :]
@@ -295,18 +298,18 @@ def tile_tokenlevelcompressor_pa_kernel(tc, h, w_kv_a, w_kv_b, w_z_a, w_z_b, b_a
         def live(t):
             return 0 <= t < TILES
 
-        for s in range(1, TILES + 3):
-            a, b, c, d = s, s - 1, s - 2, s - 3
+        for s in range(1, TILES + 4):
+            a, b, c, d, e = s, s - 1, s - 2, s - 3, s - 4
+            if live(e):
+                add_fold(e, 4)
+                if live(d):
+                    add_fold_on_gpsimd(e, 2)
             if live(d):
                 weigh_a(d)
                 weigh_b(d)
-                weigh_b_first(d)
             if live(a):
                 transpose_half(a, 0)
                 quantise_h(a, 0)
-            if live(d):
-                add_fold(d, 4)
-            if live(a):
                 quantise_h(a, 1)
             if live(b):
                 project(b, Z_B)
@@ -314,14 +317,14 @@ def tile_tokenlevelcompressor_pa_kernel(tc, h, w_kv_a, w_kv_b, w_z_a, w_z_b, b_a
                 move_logits(b)
             if live(c):
                 subtract_max(c)
-            if live(d) and d < TILES - 1:
-                add_fold(d, 2)
+            if live(d):
+                weigh_b_first(d)
             if live(a):
                 transpose_half(a, 1)
             if live(b):
                 max_first(b)
-            if live(d) and d < TILES - 1:
-                add_last(d)
+            if live(e) and e < TILES - 1:
+                add_last(e)
             if live(a):
                 quantise_h(a, 2)
             if live(b):

@@ -266,12 +266,12 @@ def tile_tokenlevelcompressor_pa_kernel(tc, h, w_kv_a, w_kv_b, w_z_a, w_z_b, b_a
             nc.scalar.copy(out=out_rows[:], in_=out_bank[t_from][:, 0 : t_to - t_from, :])
             nc.sync.dma_start(out=out_rows_of_tiles[:, t_from:t_to, :], in_=out_rows[:])
 
+        load_weight(Z_B)
+        load_weight(Z_A)
         load_h(0, 0)
         load_h(0, 1)
         nc.sync.dma_start(out=bias_rows[0:BLOCK, :], in_=b_b)
         nc.sync.dma_start(out=bias_rows[BLOCK:WINDOW, :], in_=b_a)
-        load_weight(Z_B)
-        load_weight(Z_A)
         load_h(1, 0)
         load_weight(C_B)
         load_weight(C_A)
@@ -279,20 +279,20 @@ def tile_tokenlevelcompressor_pa_kernel(tc, h, w_kv_a, w_kv_b, w_z_a, w_z_b, b_a
         load_h(2, 0)
         load_h(2, 1)
 
+        regroup_weight(Z_B)
+        quantise_weight(Z_B)
+        regroup_weight(Z_A)
+        quantise_weight(Z_A)
         transpose_half(0, 0)
         quantise_h(0, 0)
         quantise_h(0, 1)
-        regroup_weight(Z_B)
         transpose_half(0, 1)
         prepare_bias()
         quantise_h(0, 2)
-        regroup_weight(Z_A)
-        quantise_weight(Z_B)
         quantise_h(0, 3)
-        quantise_weight(Z_A)
         regroup_weight(C_B)
-        regroup_weight(C_A)
         quantise_weight(C_B)
+        regroup_weight(C_A)
         quantise_weight(C_A)
 
         def live(t):

@@ -101,8 +101,8 @@ def tile_tokenlevelcompressor_pa_kernel(tc, h, w_kv_a, w_kv_b, w_z_a, w_z_b, b_a
             nc.vector.tensor_copy(out=bias[:], in_=bias_bank[:, 0, 0:WINDOW])
 
         w_grouped = const.tile([P, 4, PASSES, FEATURES, PACK], BF16, name="w_grouped", align_bytes=64)
-        w_codes = const.tile([P, 4, PASSES, FEATURES], U32, name="w_codes", align_bytes=64)
-        w_scales = const.tile([P, 4, PASSES, FEATURES], U8, name="w_scales", align_bytes=64)
+        w_codes = const.tile([P, 4, PASSES, FEATURES], U32, name="w_codes", align_bytes=256)
+        w_scales = const.tile([P, 4, PASSES, FEATURES], U8, name="w_scales", align_bytes=256)
 
         def regroup_weight(j):
             nc.vector.tensor_copy(out=w_grouped[:, j], in_=w_raw[:, j].rearrange("p g t c -> p g c t"))
@@ -116,8 +116,8 @@ def tile_tokenlevelcompressor_pa_kernel(tc, h, w_kv_a, w_kv_b, w_z_a, w_z_b, b_a
 
         def transpose_half(t, half):
             if half == 0:
-                h_codes[t] = quant.tile([P, PASSES, TOKENS], U32, name="h_codes", align_bytes=64)
-                h_scales[t] = quant.tile([P, PASSES, TOKENS], U8, name="h_scales", align_bytes=64)
+                h_codes[t] = quant.tile([P, PASSES, TOKENS], U32, name="h_codes", align_bytes=256)
+                h_scales[t] = quant.tile([P, PASSES, TOKENS], U8, name="h_scales", align_bytes=256)
             words = h_half[(t, half)][:].bitcast(F32)
             for g in range(PASSES):
                 bank = tr_psum.tile([P, HALF, 2, P], F32, tag="tr", name="bank")

@@ -47,7 +47,7 @@ def tile_tokenlevelcompressor_pa_kernel(tc, h, w_kv_a, w_kv_b, w_z_a, w_z_b, b_a
         hin = ctx.enter_context(tc.tile_pool(name="hin", bufs=2 * AHEAD))
         grp = ctx.enter_context(tc.tile_pool(name="grp", bufs=2 * PASSES))
         quant = ctx.enter_context(tc.tile_pool(name="quant", bufs=3))
-        soft = ctx.enter_context(tc.tile_pool(name="soft", bufs=3))
+        soft = ctx.enter_context(tc.tile_pool(name="soft", bufs=2))
         tr_psum = ctx.enter_context(tc.psum_pool(name="tr_psum", bufs=4))
         acc_psum = ctx.enter_context(tc.psum_pool(name="acc_psum", bufs=1))
         ctx.enter_context(tc.manual_schedule())
@@ -59,6 +59,7 @@ def tile_tokenlevelcompressor_pa_kernel(tc, h, w_kv_a, w_kv_b, w_z_a, w_z_b, b_a
         banks = {}
         top = {}
         ep = {}
+        part = {}
 
         def load_h(t, half):
             h_half[(t, half)] = hin.tile([P, HALF * D], BF16, name="h_half")
@@ -66,6 +67,14 @@ def tile_tokenlevelcompressor_pa_kernel(tc, h, w_kv_a, w_kv_b, w_z_a, w_z_b, b_a
                 out=h_half[(t, half)][:].rearrange("p (i k) -> p i k", i=HALF),
                 in_=h_tiles[t][:, half * HALF : (half + 1) * HALF, :],
             )
+
+        def load_first_h(half):
+            h_half[(0, half)] = hin.tile([P, HALF * D], BF16, name="h_half")
+            for g in range(PASSES):
+                nc.sync.dma_start(
+                    out=h_half[(0, half)][:].rearrange("p (i k) -> p i k", i=HALF)[:, :, g * K_PASS : (g + 1) * K_PASS],
+                    in_=h_tiles[0][:, half * HALF : (half + 1) * HALF, g * K_PASS : (g + 1) * K_PASS],
+                )
 
         w_raw = const.tile([P, 4, PASSES, PACK, FEATURES], BF16, name="w_raw")
 
@@ -228,19 +237,23 @@ def tile_tokenlevelcompressor_pa_kernel(tc, h, w_kv_a, w_kv_b, w_z_a, w_z_b, b_a
             )
 
         def add_fold(t, n):
-            nc.vector.tensor_add(out=ep[t][:, :, 0:n], in0=ep[t][:, :, 0:n], in1=ep[t][:, :, n : 2 * n])
+            nc.vector.tensor_add(out=part[t][:, :, 0:n], in0=part[t][:, :, 0:n], in1=part[t][:, :, n : 2 * n])
 
         sums = const.tile([P, 2, TILES * TILE_BLOCKS], F32, name="sums")
         inverse_root = const.tile([P, TILES * TILE_BLOCKS], F32, name="inverse_root")
         inverse = const.tile([P, TILES * TILE_BLOCKS], F32, name="inverse")
         result = const.tile([P, TILES * TILE_BLOCKS], F32, name="result")
 
-        def add_fold_on_gpsimd(t, n):
-            nc.gpsimd.tensor_add(out=ep[t][:, :, 0:n], in0=ep[t][:, :, 0:n], in1=ep[t][:, :, n : 2 * n])
+        def add_exponentials_on_gpsimd(t):
+            part[t] = soft.tile([P, 2, BLOCK, TILE_BLOCKS], F32, name="part")
+            nc.gpsimd.tensor_add(out=part[t][:, 0], in0=ep[t][:, 0, 0:BLOCK], in1=ep[t][:, 0, BLOCK:WINDOW])
+
+        def add_products(t):
+            nc.vector.tensor_add(out=part[t][:, 1], in0=ep[t][:, 1, 0:BLOCK], in1=ep[t][:, 1, BLOCK:WINDOW])
 
         def add_last(t):
             nc.vector.tensor_add(
-                out=sums[:, :, t * TILE_BLOCKS : (t + 1) * TILE_BLOCKS], in0=ep[t][:, :, 0, :], in1=ep[t][:, :, 1, :]
+                out=sums[:, :, t * TILE_BLOCKS : (t + 1) * TILE_BLOCKS], in0=part[t][:, :, 0, :], in1=part[t][:, :, 1, :]
             )
 
         def invert(t_from, t_to):
@@ -268,15 +281,15 @@ def tile_tokenlevelcompressor_pa_kernel(tc, h, w_kv_a, w_kv_b, w_z_a, w_z_b, b_a
 
         load_weight(Z_B)
         load_weight(Z_A)
-        load_h(0, 0)
-        load_h(0, 1)
+        load_first_h(0)
+        load_first_h(1)
         nc.sync.dma_start(out=bias_rows[0:BLOCK, :], in_=b_b)
         nc.sync.dma_start(out=bias_rows[BLOCK:WINDOW, :], in_=b_a)
         load_h(1, 0)
-        load_weight(C_B)
-        load_weight(C_A)
         load_h(1, 1)
         load_h(2, 0)
+        load_weight(C_B)
+        load_weight(C_A)
         load_h(2, 1)
 
         regroup_weight(Z_B)
@@ -290,49 +303,52 @@ def tile_tokenlevelcompressor_pa_kernel(tc, h, w_kv_a, w_kv_b, w_z_a, w_z_b, b_a
         prepare_bias()
         quantise_h(0, 2)
         quantise_h(0, 3)
-        regroup_weight(C_B)
-        quantise_weight(C_B)
-        regroup_weight(C_A)
-        quantise_weight(C_A)
 
         def live(t):
             return 0 <= t < TILES
 
-        for s in range(1, TILES + 4):
-            a, b, c, d, e = s, s - 1, s - 2, s - 3, s - 4
-            if live(e):
-                add_fold(e, 4)
-                if live(d):
-                    add_fold_on_gpsimd(e, 2)
+        for s in range(1, TILES + 3):
+            a, b, c, d = s, s - 1, s - 2, s - 3
             if live(d):
+                add_exponentials_on_gpsimd(d)
                 weigh_a(d)
                 weigh_b(d)
             if live(a):
                 transpose_half(a, 0)
                 quantise_h(a, 0)
+            if live(d):
+                weigh_b_first(d)
+            if live(a):
                 quantise_h(a, 1)
             if live(b):
                 project(b, Z_B)
                 project(b, Z_A)
                 move_logits(b)
+            if live(d):
+                add_products(d)
             if live(c):
                 subtract_max(c)
-            if live(d):
-                weigh_b_first(d)
             if live(a):
                 transpose_half(a, 1)
+            if live(d) and d < TILES - 1:
+                add_fold(d, 2)
             if live(b):
                 max_first(b)
-            if live(e) and e < TILES - 1:
-                add_last(e)
             if live(a):
                 quantise_h(a, 2)
             if live(b):
                 max_fold(b, 2)
+            if live(d) and d < TILES - 1:
+                add_last(d)
             if live(a):
                 quantise_h(a, 3)
             if live(b):
                 max_fold(b, 1)
+            if s == 1:
+                regroup_weight(C_B)
+                quantise_weight(C_B)
+                regroup_weight(C_A)
+                quantise_weight(C_A)
             if live(c):
                 project(c, C_B)
                 project(c, C_A)

@@ -48,8 +48,8 @@ def tile_tokenlevelcompressor_pa_kernel(tc, h, w_kv_a, w_kv_b, w_z_a, w_z_b, b_a
         grp = ctx.enter_context(tc.tile_pool(name="grp", bufs=2 * PASSES))
         quant = ctx.enter_context(tc.tile_pool(name="quant", bufs=3))
         soft = ctx.enter_context(tc.tile_pool(name="soft", bufs=2))
-        tr_psum = ctx.enter_context(tc.psum_pool(name="tr_psum", bufs=4))
-        acc_psum = ctx.enter_context(tc.psum_pool(name="acc_psum", bufs=1))
+        tr_psum = ctx.enter_context(tc.psum_pool(name="tr_psum", bufs=5))
+        acc_psum = ctx.enter_context(tc.psum_pool(name="acc_psum", bufs=3))
         ctx.enter_context(tc.manual_schedule())
 
         h_half = {}
@@ -153,7 +153,7 @@ def tile_tokenlevelcompressor_pa_kernel(tc, h, w_kv_a, w_kv_b, w_z_a, w_z_b, b_a
                 )
 
         def project(t, j):
-            banks[(t, j)] = acc_psum.tile([P, TOKENS], F32, tag=bank_names[j], name=bank_names[j])
+            banks[(t, j)] = acc_psum.tile([P, TOKENS], F32, tag="acc", name=bank_names[j])
             for g in range(PASSES):
                 nc.tensor.matmul_mx(
                     out=banks[(t, j)][:],
@@ -311,8 +311,8 @@ def tile_tokenlevelcompressor_pa_kernel(tc, h, w_kv_a, w_kv_b, w_z_a, w_z_b, b_a
             a, b, c, d = s, s - 1, s - 2, s - 3
             if live(d):
                 add_exponentials_on_gpsimd(d)
-                weigh_a(d)
                 weigh_b(d)
+                weigh_a(d)
             if live(a):
                 transpose_half(a, 0)
                 quantise_h(a, 0)

from contextlib import ExitStack

import concourse.mybir as mybir
from concourse.masks import make_identity

F32 = mybir.dt.float32
BF16 = mybir.dt.bfloat16
U32 = mybir.dt.uint32
U8 = mybir.dt.uint8
FP8X4 = mybir.dt.float8_e4m3fn_x4
ACT = mybir.ActivationFunctionType

P = 128
PACK = 4
K_PASS = P * PACK
D = 2048
PASSES = D // K_PASS
FEATURES = 128
BLOCK = 4
WINDOW = 2 * BLOCK
TILE_BLOCKS = P
TOKENS = TILE_BLOCKS * BLOCK
SEQUENCES = 4
SEQ_TILES = 2
TILES = SEQUENCES * SEQ_TILES
HALF = BLOCK // 2
WORDS = D // 2
HALF_TOKENS = HALF * TILE_BLOCKS
BANK_SQUARES = 4
ROW = 264
NEG = -3.4028234663852886e38
AHEAD = 3

FLOPS = 2 * SEQUENCES * 1024 * D * 4 * FEATURES


def tile_tokenlevelcompressor_pa_kernel(tc, h, w_kv_a, w_kv_b, w_z_a, w_z_b, b_a, b_b, out):
    nc = tc.nc
    h_tiles = h.rearrange("n (t p i) k -> (n t) p i k", t=SEQ_TILES, p=P, i=BLOCK)
    out_rows_of_tiles = out.rearrange("n (t j) f -> j (n t) f", t=SEQ_TILES)
    weights = (w_z_b, w_z_a, w_kv_b, w_kv_a)
    Z_B, Z_A, C_B, C_A = 0, 1, 2, 3
    bank_names = ("z_b", "z_a", "c_b", "c_a")

    with ExitStack() as ctx:
        const = ctx.enter_context(tc.tile_pool(name="const", bufs=1))
        hin = ctx.enter_context(tc.tile_pool(name="hin", bufs=2 * AHEAD))
        grp = ctx.enter_context(tc.tile_pool(name="grp", bufs=2 * PASSES))
        quant = ctx.enter_context(tc.tile_pool(name="quant", bufs=3))
        soft = ctx.enter_context(tc.tile_pool(name="soft", bufs=2))
        tr_psum = ctx.enter_context(tc.psum_pool(name="tr_psum", bufs=5))
        acc_psum = ctx.enter_context(tc.psum_pool(name="acc_psum", bufs=3))
        ctx.enter_context(tc.manual_schedule())

        h_half = {}
        grouped = {}
        h_codes = {}
        h_scales = {}
        banks = {}
        top = {}
        ep = {}
        part = {}

        def load_h(t, half):
            h_half[(t, half)] = hin.tile([P, HALF * D], BF16, name="h_half")
            nc.sync.dma_start(
                out=h_half[(t, half)][:].rearrange("p (i k) -> p i k", i=HALF),
                in_=h_tiles[t][:, half * HALF : (half + 1) * HALF, :],
            )

        def load_first_h(half):
            h_half[(0, half)] = hin.tile([P, HALF * D], BF16, name="h_half")
            for g in range(PASSES):
                nc.sync.dma_start(
                    out=h_half[(0, half)][:].rearrange("p (i k) -> p i k", i=HALF)[:, :, g * K_PASS : (g + 1) * K_PASS],
                    in_=h_tiles[0][:, half * HALF : (half + 1) * HALF, g * K_PASS : (g + 1) * K_PASS],
                )

        w_raw = const.tile([P, 4, PASSES, PACK, FEATURES], BF16, name="w_raw")

        def load_weight(j):
            nc.sync.dma_start(
                out=w_raw[:, j].rearrange("p g (u e) c -> p (g u) (e c)", u=2, e=2),
                in_=weights[j].rearrange("(s p e) c -> p s (e c)", s=2 * PASSES, p=P, e=2),
            )

        bias_rows = const.tile([P, P], BF16, name="bias_rows")
        bias_rows32 = const.tile([P, P], F32, name="bias_rows32")
        bias = const.tile([P, WINDOW], F32, name="bias")
        nc.vector.memset(bias_rows[:], 0.0)

        ident = const.tile([P, P], F32, name="ident")
        make_identity(nc, ident[:])

        table_seed = const.tile([P, 1], F32, name="table_seed")
        table_out = const.tile([P, 1], F32, name="table_out")
        nc.vector.memset(table_seed[:], 0.0)
        nc.scalar.activation(out=table_out[:], in_=table_seed[:], func=ACT.Exp)

        logits = [const.tile([P, WINDOW, ROW], F32, name="logits%d" % q) for q in range(2)]
        carry = [const.tile([P, BLOCK, 1], F32, name="carry%d" % q) for q in range(2)]
        nc.vector.memset(carry[0][:], 0.0)
        for q in range(2):
            nc.vector.memset(logits[q][:, 0:BLOCK, 0:8], NEG)

        def prepare_bias():
            nc.vector.tensor_copy(out=bias_rows32[:], in_=bias_rows[:])
            bias_bank = tr_psum.tile([P, BANK_SQUARES, P], F32, tag="tr", name="bias_bank")
            nc.tensor.transpose(bias_bank[:, 0, :], bias_rows32[:], ident[:])
            nc.vector.tensor_copy(out=bias[:], in_=bias_bank[:, 0, 0:WINDOW])

        w_grouped = const.tile([P, 4, PASSES, FEATURES, PACK], BF16, name="w_grouped", align_bytes=64)
        w_codes = const.tile([P, 4, PASSES, FEATURES], U32, name="w_codes", align_bytes=256)
        w_scales = const.tile([P, 4, PASSES, FEATURES], U8, name="w_scales", align_bytes=256)

        def regroup_weight(j):
            nc.vector.tensor_copy(out=w_grouped[:, j], in_=w_raw[:, j].rearrange("p g t c -> p g c t"))

        def quantise_weight(j):
            nc.vector.quantize_mx(
                out=w_codes[:, j].rearrange("p g c -> p (g c)").bitcast(FP8X4),
                scales=w_scales[:, j].rearrange("p g c -> p (g c)"),
                in_=w_grouped[:, j].rearrange("p g c t -> p (g c t)"),
            )

        def transpose_half(t, half):
            if half == 0:
                h_codes[t] = quant.tile([P, PASSES, TOKENS], U32, name="h_codes", align_bytes=256)
                h_scales[t] = quant.tile([P, PASSES, TOKENS], U8, name="h_scales", align_bytes=256)
            words = h_half[(t, half)][:].bitcast(F32)
            for g in range(PASSES):
                bank = tr_psum.tile([P, HALF, 2, P], F32, tag="tr", name="bank")
                for a in range(HALF):
                    for u in range(2):
                        first = a * WORDS + g * 2 * P + u * P
                        nc.tensor.transpose(bank[:, a, u, :], words[:, first : first + P], ident[:])
                grouped[(t, half, g)] = grp.tile([P, HALF_TOKENS * PACK], BF16, name="grouped", align_bytes=64)
                nc.scalar.copy(
                    out=grouped[(t, half, g)][:].bitcast(F32).rearrange("p (a r u) -> p a r u", a=HALF, u=2),
                    in_=bank[:].rearrange("p a u r -> p a r u"),
                )
            if t + AHEAD < TILES:
                load_h(t + AHEAD, half)

        def quantise_h(t, quarter):
            half, pass_pair = divmod(quarter, 2)
            cols = slice(half * HALF_TOKENS, (half + 1) * HALF_TOKENS)
            for g in (2 * pass_pair, 2 * pass_pair + 1):
                nc.vector.quantize_mx(
                    out=h_codes[t][:, g, cols].bitcast(FP8X4),
                    scales=h_scales[t][:, g, cols],
                    in_=grouped[(t, half, g)][:],
                )

        def project(t, j):
            banks[(t, j)] = acc_psum.tile([P, TOKENS], F32, tag="acc", name=bank_names[j])
            for g in range(PASSES):
                nc.tensor.matmul_mx(
                    out=banks[(t, j)][:],
                    lhsT=w_codes[:, j, g, :].bitcast(FP8X4),
                    lhsT_scale=w_scales[:, j, g, :],
                    rhs=h_codes[t][:, g, :].bitcast(FP8X4),
                    rhs_scale=h_scales[t][:, g, :],
                    start=(g == 0),
                    stop=(g == PASSES - 1),
                )

        def place(t):
            return (t // SEQ_TILES) % 2, (t % SEQ_TILES) * TILE_BLOCKS

        def move_logits(t):
            q, first = place(t)
            for i in range(BLOCK):
                nc.scalar.activation(
                    out=logits[q][:, i, first + 1 : first + 1 + TILE_BLOCKS],
                    in_=banks[(t, Z_B)][:, i * TILE_BLOCKS : (i + 1) * TILE_BLOCKS],
                    func=ACT.Identity,
                    bias=bias[:, i : i + 1],
                    scale=1.0,
                )
            for i in range(BLOCK):
                nc.scalar.activation(
                    out=logits[q][:, BLOCK + i, first : first + TILE_BLOCKS],
                    in_=banks[(t, Z_A)][:, i * TILE_BLOCKS : (i + 1) * TILE_BLOCKS],
                    func=ACT.Identity,
                    bias=bias[:, BLOCK + i : BLOCK + i + 1],
                    scale=1.0,
                )

        def keep_last_values_b(t):
            nc.scalar.copy(
                out=carry[1][:],
                in_=banks[(t, C_B)][:].rearrange("p (i j) -> p i j", i=BLOCK)[:, :, TILE_BLOCKS - 1 : TILE_BLOCKS],
            )

        def max_first(t):
            q, first = place(t)
            top[t] = soft.tile([P, BLOCK, TILE_BLOCKS], F32, name="top")
            nc.vector.tensor_max(
                out=top[t][:],
                in0=logits[q][:, 0:BLOCK, first : first + TILE_BLOCKS],
                in1=logits[q][:, BLOCK:WINDOW, first : first + TILE_BLOCKS],
            )

        def max_fold(t, n):
            nc.vector.tensor_max(out=top[t][:, 0:n, :], in0=top[t][:, 0:n, :], in1=top[t][:, n : 2 * n, :])

        def subtract_max(t):
            q, first = place(t)
            ep[t] = soft.tile([P, 2, WINDOW, TILE_BLOCKS], F32, name="ep")
            nc.vector.tensor_sub(
                out=ep[t][:, 0],
                in0=logits[q][:, :, first : first + TILE_BLOCKS],
                in1=top[t][:, 0:1, :].to_broadcast([P, WINDOW, TILE_BLOCKS]),
            )

        def exponentials(t):
            nc.scalar.activation(out=ep[t][:, 0], in_=ep[t][:, 0], func=ACT.Exp)

        def weigh_a(t):
            nc.vector.tensor_mul(
                out=ep[t][:, 1, BLOCK:WINDOW],
                in0=ep[t][:, 0, BLOCK:WINDOW],
                in1=banks[(t, C_A)][:].rearrange("p (i j) -> p i j", i=BLOCK),
            )

        def weigh_b(t):
            nc.vector.tensor_mul(
                out=ep[t][:, 1, 0:BLOCK, 1:TILE_BLOCKS],
                in0=ep[t][:, 0, 0:BLOCK, 1:TILE_BLOCKS],
                in1=banks[(t, C_B)][:].rearrange("p (i j) -> p i j", i=BLOCK)[:, :, 0 : TILE_BLOCKS - 1],
            )

        def weigh_b_first(t):
            nc.vector.tensor_mul(
                out=ep[t][:, 1, 0:BLOCK, 0:1], in0=ep[t][:, 0, 0:BLOCK, 0:1], in1=carry[t % SEQ_TILES][:]
            )

        def add_fold(t, n):
            nc.vector.tensor_add(out=part[t][:, :, 0:n], in0=part[t][:, :, 0:n], in1=part[t][:, :, n : 2 * n])

        sums = const.tile([P, 2, TILES * TILE_BLOCKS], F32, name="sums")
        inverse_root = const.tile([P, TILES * TILE_BLOCKS], F32, name="inverse_root")
        inverse = const.tile([P, TILES * TILE_BLOCKS], F32, name="inverse")
        result = const.tile([P, TILES * TILE_BLOCKS], F32, name="result")

        def add_exponentials_on_gpsimd(t):
            part[t] = soft.tile([P, 2, BLOCK, TILE_BLOCKS], F32, name="part")
            nc.gpsimd.tensor_add(out=part[t][:, 0], in0=ep[t][:, 0, 0:BLOCK], in1=ep[t][:, 0, BLOCK:WINDOW])

        def add_products(t):
            nc.vector.tensor_add(out=part[t][:, 1], in0=ep[t][:, 1, 0:BLOCK], in1=ep[t][:, 1, BLOCK:WINDOW])

        def add_last(t):
            nc.vector.tensor_add(
                out=sums[:, :, t * TILE_BLOCKS : (t + 1) * TILE_BLOCKS], in0=part[t][:, :, 0, :], in1=part[t][:, :, 1, :]
            )

        def invert(t_from, t_to):
            cols = slice(t_from * TILE_BLOCKS, t_to * TILE_BLOCKS)
            nc.scalar.activation(out=inverse_root[:, cols], in_=sums[:, 0, cols], func=ACT.Abs_reciprocal_sqrt)
            nc.scalar.activation(out=inverse[:, cols], in_=inverse_root[:, cols], func=ACT.Square)

        def divide(t_from, t_to):
            cols = slice(t_from * TILE_BLOCKS, t_to * TILE_BLOCKS)
            nc.vector.tensor_mul(out=result[:, cols], in0=sums[:, 1, cols], in1=inverse[:, cols])

        out_bank = {}

        def transpose_out(t_from, t_to):
            out_bank[t_from] = tr_psum.tile([P, BANK_SQUARES, FEATURES], F32, tag="tr", name="out_bank")
            for t in range(t_from, t_to):
                nc.tensor.transpose(
                    out_bank[t_from][:, t - t_from, :], result[:, t * TILE_BLOCKS : (t + 1) * TILE_BLOCKS], ident[:]
                )

        def store(t_from, t_to):
            out_rows = const.tile([P, t_to - t_from, FEATURES], F32, name="out_rows%d" % t_from)
            nc.scalar.copy(out=out_rows[:], in_=out_bank[t_from][:, 0 : t_to - t_from, :])
            nc.sync.dma_start(out=out_rows_of_tiles[:, t_from:t_to, :], in_=out_rows[:])

        load_weight(Z_B)
        load_weight(Z_A)
        load_first_h(0)
        load_first_h(1)
        nc.sync.dma_start(out=bias_rows[0:BLOCK, :], in_=b_b)
        nc.sync.dma_start(out=bias_rows[BLOCK:WINDOW, :], in_=b_a)
        load_h(1, 0)
        load_h(1, 1)
        load_h(2, 0)
        load_weight(C_B)
        load_weight(C_A)
        load_h(2, 1)

        regroup_weight(Z_B)
        quantise_weight(Z_B)
        regroup_weight(Z_A)
        quantise_weight(Z_A)
        transpose_half(0, 0)
        quantise_h(0, 0)
        quantise_h(0, 1)
        transpose_half(0, 1)
        prepare_bias()
        quantise_h(0, 2)
        quantise_h(0, 3)

        def live(t):
            return 0 <= t < TILES

        for s in range(1, TILES + 3):
            a, b, c, d = s, s - 1, s - 2, s - 3
            if live(d):
                add_exponentials_on_gpsimd(d)
                weigh_b(d)
                weigh_a(d)
            if live(a):
                transpose_half(a, 0)
                quantise_h(a, 0)
            if live(d):
                weigh_b_first(d)
            if live(a):
                quantise_h(a, 1)
            if live(b):
                project(b, Z_B)
                project(b, Z_A)
                move_logits(b)
            if live(d):
                add_products(d)
            if live(c):
                subtract_max(c)
            if live(a):
                transpose_half(a, 1)
            if live(d) and d < TILES - 1:
                add_fold(d, 2)
            if live(b):
                max_first(b)
            if live(a):
                quantise_h(a, 2)
            if live(b):
                max_fold(b, 2)
            if live(d) and d < TILES - 1:
                add_last(d)
            if live(a):
                quantise_h(a, 3)
            if live(b):
                max_fold(b, 1)
            if s == 1:
                regroup_weight(C_B)
                quantise_weight(C_B)
                regroup_weight(C_A)
                quantise_weight(C_A)
            if live(c):
                project(c, C_B)
                project(c, C_A)
                exponentials(c)
                if c % SEQ_TILES == 0:
                    keep_last_values_b(c)

        last = TILES - 1
        invert(0, BANK_SQUARES)
        invert(BANK_SQUARES, last)
        divide(0, BANK_SQUARES)
        add_fold(last, 2)
        transpose_out(0, BANK_SQUARES)
        store(0, BANK_SQUARES)
        divide(BANK_SQUARES, last)
        add_last(last)
        transpose_out(BANK_SQUARES, last)
        invert(last, TILES)
        store(BANK_SQUARES, last)
        divide(last, TILES)
        transpose_out(last, TILES)
        store(last, TILES)
